import numpy as np
import ml_dtypes


def mxq(x, axis, fmt="e4m3"):
    dtype, down = {"e4m3": (ml_dtypes.float8_e4m3fn, 7), "e5m2": (ml_dtypes.float8_e5m2, 14)}[fmt]
    v = np.moveaxis(np.asarray(x, np.float32).astype(ml_dtypes.bfloat16).astype(np.float64), axis, -1)
    blocks = v.reshape(v.shape[:-1] + (-1, 32))
    amax = np.abs(blocks).max(-1, keepdims=True)
    byte = np.maximum(np.where(amax > 0, np.frexp(amax)[1] - 1 + 127, 0) - down, 1)
    scale = np.exp2(byte - 127.0)
    codes = (blocks / scale).astype(np.float32).astype(dtype).astype(np.float64)
    return np.moveaxis((codes * scale).reshape(v.shape), -1, axis)


WIDE = False


def mx_kscale(k):
    if not WIDE:
        return np.ones(k)
    levels = np.array([10, -10, 5, -5, 0])
    a = np.random.permutation(np.resize(levels, k // 512 * 4)).reshape(k // 512, 4)
    idx = np.arange(k)
    return np.exp2(a[idx // 512, idx % 128 // 32])


BF16 = ml_dtypes.bfloat16


def bf(x):
    return np.asarray(x, np.float32).astype(BF16)


def f64(x):
    return np.asarray(x).astype(np.float64)


B, L, LV, H = 32, 32, 64, 1024
NUM_ITERATIONS = 3
X = 0.25
V = 0.12 * L
A = 0.6 / (np.sqrt(H) * V)


def setup_inputs():
    s = mx_kscale(H)
    return {"text_feat": bf(np.random.standard_normal((B, L, H)) * X * s),
            "vision_proj": bf(np.random.standard_normal((B, 1, H)) * V),
            "Wt": bf(np.random.standard_normal((H, H)) * A / (X * np.sqrt(H)) / s[None, :]),
            "bt": bf(np.random.standard_normal(H) * 0.5 * A)}


def reference(text_feat, vision_proj, Wt, bt):
    vp = f64(vision_proj)
    text_proj = (mxq(f64(text_feat), 2, "e4m3") @ mxq(f64(Wt), 1, "e4m3").T) + f64(bt)
    agreement = np.sum(text_proj * vp, axis=-1, keepdims=True)
    coupling = np.zeros_like(agreement)
    for _ in range(NUM_ITERATIONS - 1):
        coupling = coupling + agreement
    e = np.exp(coupling - coupling.max(axis=1, keepdims=True))
    routing_weights = e / e.sum(axis=1, keepdims=True)
    weighted_vision = routing_weights * vp
    return text_proj, weighted_vision

@@ -1,0 +1,220 @@
+from contextlib import ExitStack
+
+import concourse.mybir as mybir
+from concourse.masks import make_identity
+
+F32 = mybir.dt.float32
+BF16 = mybir.dt.bfloat16
+U32 = mybir.dt.uint32
+U8 = mybir.dt.uint8
+FP8X4 = mybir.dt.float8_e4m3fn_x4
+ALU = mybir.AluOpType
+ACT = mybir.ActivationFunctionType
+AXIS = mybir.AxisListType
+
+P = 128
+BATCH = 32
+TOKENS = 32
+H = 1024
+
+K_PASS = 4 * P
+PASSES = H // K_PASS
+CHUNKS = H // (2 * P)
+N_HALF = 512
+HALVES = H // N_HALF
+BLOCKS_PER_HALF = N_HALF // P
+
+BATCHES_PER_TILE = 16
+ROWS_PER_BATCH = P // BATCHES_PER_TILE
+TILES_PER_GROUP = TOKENS // ROWS_PER_BATCH
+GROUPS = BATCH // BATCHES_PER_TILE
+
+FLOPS = 2 * BATCH * TOKENS * H * H
+
+
+def tile_dynamicroutingfusion_pa_kernel(tc, text_feat, vision_proj, Wt, bt, out_0, out_1):
+    nc = tc.nc
+
+    x_dram = text_feat.flatten_outer_dims().rearrange("(g p t) k -> g p t k", p=P, t=TILES_PER_GROUP)
+    proj_dram = out_0.flatten_outer_dims().rearrange("(g p t) h -> g p t h", p=P, t=TILES_PER_GROUP)
+    weighted_dram = out_1.flatten_outer_dims().rearrange("(g p t) h -> g p t h", p=P, t=TILES_PER_GROUP)
+    w_dram = Wt.rearrange("(j p) k -> j p k", p=P)
+
+    with ExitStack() as ctx:
+        keep = ctx.enter_context(tc.tile_pool(name="keep", bufs=1))
+        stage = ctx.enter_context(tc.tile_pool(name="stage", bufs=3))
+        results = ctx.enter_context(tc.tile_pool(name="results", bufs=6))
+        small = ctx.enter_context(tc.tile_pool(name="small", bufs=2))
+        psum_t = ctx.enter_context(tc.psum_pool(name="psum_t", bufs=3))
+        psum_acc = ctx.enter_context(tc.psum_pool(name="psum_acc", bufs=4))
+        psum_s = ctx.enter_context(tc.psum_pool(name="psum_s", bufs=1))
+
+        x_raw = keep.tile([P, GROUPS, TILES_PER_GROUP, H], BF16)
+        w_raw = keep.tile([P, HALVES, BLOCKS_PER_HALF, H], BF16)
+        vision_rows = keep.tile([P, GROUPS, H], BF16)
+        bias_seed = keep.tile([P, H], BF16)
+        bias_rows = keep.tile([P, H], BF16)
+        x_codes = keep.tile([P, GROUPS, TILES_PER_GROUP, PASSES * P], U32, align_bytes=64)
+        x_scales = keep.tile([P, GROUPS, TILES_PER_GROUP, PASSES * P], U8, align_bytes=64)
+        w_codes = keep.tile([P, HALVES, PASSES * N_HALF], U32, align_bytes=64)
+        w_scales = keep.tile([P, HALVES, PASSES * N_HALF], U8, align_bytes=64)
+
+        nc.vector.memset(bias_seed[:], 0.0)
+        nc.sync.dma_start(out=bias_seed[0:1, :], in_=bt.unsqueeze(0))
+
+        def load_x(g, t):
+            nc.sync.dma_start(out=x_raw[:, g, t, :], in_=x_dram[g, :, t, :])
+
+        def load_w(half):
+            for j in range(BLOCKS_PER_HALF):
+                nc.sync.dma_start(out=w_raw[:, half, j, :], in_=w_dram[half * BLOCKS_PER_HALF + j])
+
+        def load_vision(g):
+            rows = vision_proj[g * BATCHES_PER_TILE : (g + 1) * BATCHES_PER_TILE, :, :]
+            nc.sync.dma_start(
+                out=vision_rows[:, g, :], in_=rows.to_broadcast([BATCHES_PER_TILE, ROWS_PER_BATCH, H])
+            )
+
+        load_x(0, 0)
+        load_w(0)
+        load_vision(0)
+        for t in range(1, TILES_PER_GROUP):
+            load_x(0, t)
+        load_w(1)
+        for g in range(1, GROUPS):
+            for t in range(TILES_PER_GROUP):
+                load_x(g, t)
+            load_vision(g)
+
+        ident = keep.tile([P, P], F32)
+        make_identity(nc, ident[:])
+        ones = keep.tile([P, P], BF16)
+        nc.vector.memset(ones[:], 1.0)
+        batch_of = keep.tile([P, BATCHES_PER_TILE], F32)
+        nc.vector.tensor_reduce(
+            out=batch_of[:], in_=ident[:].rearrange("p (b j) -> p b j", j=ROWS_PER_BATCH), axis=AXIS.X, op=ALU.add
+        )
+        same_batch = keep.tile([P, P], F32)
+        nc.vector.tensor_copy(
+            out=same_batch[:].rearrange("p (b j) -> p b j", j=ROWS_PER_BATCH),
+            in_=batch_of[:].unsqueeze(2).to_broadcast([P, BATCHES_PER_TILE, ROWS_PER_BATCH]),
+        )
+        place_of = keep.tile([P, ROWS_PER_BATCH], F32)
+        nc.vector.tensor_reduce(
+            out=place_of[:], in_=ident[:].rearrange("p (b j) -> p j b", j=ROWS_PER_BATCH), axis=AXIS.X, op=ALU.add
+        )
+        warm = keep.tile([P, 1], F32)
+        nc.vector.memset(warm[:], 0.0)
+        nc.scalar.activation(out=warm[:], in_=warm[:], func=ACT.Exp)
+
+        bias_bank = psum_t.tile([P, H], BF16, tag="bank")
+        for half in range(HALVES):
+            cols = slice(half * N_HALF, (half + 1) * N_HALF)
+            nc.tensor.matmul(out=bias_bank[:, cols], lhsT=ones[:], rhs=bias_seed[:, cols], start=True, stop=True)
+        nc.scalar.copy(out=bias_rows[:], in_=bias_bank[:])
+
+        def transpose_rows(raw_rows):
+            words = raw_rows.bitcast(F32)
+            bank = psum_t.tile([P, CHUNKS, P], F32, tag="bank")
+            for c in range(CHUNKS):
+                nc.tensor.transpose(bank[:, c, :], words[:, c * P : (c + 1) * P], ident[:])
+            return bank[:].rearrange("p (g u) r -> p g r u", u=2)
+
+        def prepare_x(g, t):
+            grouped = stage.tile([P, PASSES * P * 4], BF16, align_bytes=64, tag="grouped_x")
+            nc.scalar.copy(
+                out=grouped[:].bitcast(F32).rearrange("p (g r u) -> p g r u", g=PASSES, u=2),
+                in_=transpose_rows(x_raw[:, g, t, :]),
+            )
+            nc.vector.quantize_mx(out=x_codes[:, g, t, :].bitcast(FP8X4), scales=x_scales[:, g, t, :], in_=grouped[:])
+
+        def prepare_w(half):
+            grouped = stage.tile([P, PASSES * N_HALF * 4], BF16, align_bytes=64, tag="grouped_w", bufs=2)
+            grouped_words = grouped[:].bitcast(F32).rearrange("p (g n u) -> p g n u", g=PASSES, u=2)
+            for j in range(BLOCKS_PER_HALF):
+                transposed = transpose_rows(w_raw[:, half, j, :])
+                if j % 2 == 0:
+                    nc.scalar.copy(out=grouped_words[:, :, j * P : (j + 1) * P, :], in_=transposed)
+                else:
+                    nc.vector.tensor_copy(out=grouped_words[:, :, j * P : (j + 1) * P, :], in_=transposed)
+            for c in range(PASSES):
+                nc.vector.quantize_mx(
+                    out=w_codes[:, half, c * N_HALF : (c + 1) * N_HALF].bitcast(FP8X4),
+                    scales=w_scales[:, half, c * N_HALF : (c + 1) * N_HALF],
+                    in_=grouped[:, c * N_HALF * 4 : (c + 1) * N_HALF * 4],
+                )
+
+        def project(g, t, half, coupling_parts):
+            cols = slice(half * N_HALF, (half + 1) * N_HALF)
+            acc = psum_acc.tile([P, N_HALF], F32)
+            for c in range(PASSES):
+                nc.tensor.matmul_mx(
+                    out=acc[:],
+                    lhsT=x_codes[:, g, t, c * P : (c + 1) * P].bitcast(FP8X4),
+                    lhsT_scale=x_scales[:, g, t, c * P : (c + 1) * P],
+                    rhs=w_codes[:, half, c * N_HALF : (c + 1) * N_HALF].bitcast(FP8X4),
+                    rhs_scale=w_scales[:, half, c * N_HALF : (c + 1) * N_HALF],
+                    start=(c == 0),
+                    stop=(c == PASSES - 1),
+                )
+            product = stage.tile([P, N_HALF], F32, tag="product")
+            nc.vector.scalar_tensor_tensor(
+                out=product[:],
+                in0=acc[:],
+                scalar=2.0,
+                in1=vision_rows[:, g, cols],
+                op0=ALU.mult,
+                op1=ALU.mult,
+                accum_out=coupling_parts[:, half, t : t + 1],
+            )
+            proj = results.tile([P, N_HALF], F32, tag="proj")
+            nc.vector.tensor_tensor(out=proj[:], in0=acc[:], in1=bias_rows[:, cols], op=ALU.add)
+            nc.sync.dma_start(out=proj_dram[g, :, t, cols], in_=proj[:])
+
+        def route(g, coupling_parts):
+            coupling = small.tile([P, TILES_PER_GROUP], F32, tag="coupling")
+            nc.vector.tensor_tensor(out=coupling[:], in0=coupling_parts[:, 0, :], in1=coupling_parts[:, 1, :], op=ALU.add)
+            spread = small.tile([P, TILES_PER_GROUP, ROWS_PER_BATCH], F32, tag="spread")
+            nc.vector.tensor_tensor(
+                out=spread[:],
+                in0=coupling[:].unsqueeze(2).to_broadcast([P, TILES_PER_GROUP, ROWS_PER_BATCH]),
+                in1=place_of[:].unsqueeze(1).to_broadcast([P, TILES_PER_GROUP, ROWS_PER_BATCH]),
+                op=ALU.mult,
+            )
+            batch_couplings = psum_s.tile([P, TOKENS], F32)
+            nc.tensor.matmul(
+                out=batch_couplings[:], lhsT=same_batch[:], rhs=spread[:].rearrange("p t j -> p (t j)"), start=True, stop=True
+            )
+            minus_max = small.tile([P, 1], F32, tag="minus_max")
+            nc.vector.tensor_reduce(out=minus_max[:], in_=batch_couplings[:], axis=AXIS.X, op=ALU.max, negate=True)
+            exp_all = small.tile([P, TOKENS], F32, tag="exp_all")
+            exp_sum = small.tile([P, 1], F32, tag="exp_sum")
+            nc.scalar.activation(
+                out=exp_all[:], in_=batch_couplings[:], func=ACT.Exp, bias=minus_max[:], scale=1.0, accum_out=exp_sum[:]
+            )
+            exp_own = small.tile([P, TILES_PER_GROUP], F32, tag="exp_own")
+            nc.scalar.activation(out=exp_own[:], in_=coupling[:], func=ACT.Exp, bias=minus_max[:], scale=1.0)
+            inverse_sum = small.tile([P, 1], F32, tag="inverse_sum")
+            nc.vector.reciprocal(out=inverse_sum[:], in_=exp_sum[:])
+            routing = small.tile([P, TILES_PER_GROUP], F32, tag="routing")
+            nc.vector.tensor_scalar(out=routing[:], in0=exp_own[:], scalar1=inverse_sum[:, 0:1], scalar2=None, op0=ALU.mult)
+            for t in range(TILES_PER_GROUP):
+                weighted = results.tile([P, H], F32, tag="weighted", bufs=4)
+                nc.scalar.activation(out=weighted[:], in_=vision_rows[:, g, :], func=ACT.Copy, scale=routing[:, t : t + 1])
+                nc.sync.dma_start(out=weighted_dram[g, :, t, :], in_=weighted[:])
+
+        prepare_x(0, 0)
+        prepare_w(0)
+        for t in range(1, TILES_PER_GROUP):
+            prepare_x(0, t)
+        prepare_w(1)
+        for g in range(1, GROUPS):
+            for t in range(TILES_PER_GROUP):
+                prepare_x(g, t)
+
+        for g in range(GROUPS):
+            coupling_parts = small.tile([P, HALVES, TILES_PER_GROUP], F32, tag="coupling_parts")
+            for half in range(HALVES):
+                for t in range(TILES_PER_GROUP):
+                    project(g, t, half, coupling_parts)
+            route(g, coupling_parts)

@@ -22,12 +22,16 @@ PASSES = H // K_PASS
 CHUNKS = H // (2 * P)
 N_HALF = 512
 HALVES = H // N_HALF
+BLOCKS = H // P
 BLOCKS_PER_HALF = N_HALF // P
 
-BATCHES_PER_TILE = 16
+BATCHES_PER_TILE = 8
 ROWS_PER_BATCH = P // BATCHES_PER_TILE
 TILES_PER_GROUP = TOKENS // ROWS_PER_BATCH
 GROUPS = BATCH // BATCHES_PER_TILE
+
+BLOCKS_BEFORE_FIRST_BANK = 1 + BLOCKS_PER_HALF + 1
+BLOCKS_PER_BANK = 2
 
 FLOPS = 2 * BATCH * TOKENS * H * H
 
@@ -35,39 +39,39 @@ FLOPS = 2 * BATCH * TOKENS * H * H
 def tile_dynamicroutingfusion_pa_kernel(tc, text_feat, vision_proj, Wt, bt, out_0, out_1):
     nc = tc.nc
 
-    x_dram = text_feat.flatten_outer_dims().rearrange("(g p t) k -> g p t k", p=P, t=TILES_PER_GROUP)
-    proj_dram = out_0.flatten_outer_dims().rearrange("(g p t) h -> g p t h", p=P, t=TILES_PER_GROUP)
-    weighted_dram = out_1.flatten_outer_dims().rearrange("(g p t) h -> g p t h", p=P, t=TILES_PER_GROUP)
+    x_dram = text_feat.flatten_outer_dims().rearrange("(g p t) k -> g t p k", p=P, t=TILES_PER_GROUP)
+    proj_dram = out_0.flatten_outer_dims().rearrange("(g p t) h -> g t p h", p=P, t=TILES_PER_GROUP)
+    weighted_dram = out_1.flatten_outer_dims().rearrange("(g p t) h -> g t p h", p=P, t=TILES_PER_GROUP)
     w_dram = Wt.rearrange("(j p) k -> j p k", p=P)
 
     with ExitStack() as ctx:
         keep = ctx.enter_context(tc.tile_pool(name="keep", bufs=1))
-        stage = ctx.enter_context(tc.tile_pool(name="stage", bufs=3))
-        results = ctx.enter_context(tc.tile_pool(name="results", bufs=6))
+        stage = ctx.enter_context(tc.tile_pool(name="stage", bufs=4))
+        results = ctx.enter_context(tc.tile_pool(name="results", bufs=2 * TILES_PER_GROUP))
         small = ctx.enter_context(tc.tile_pool(name="small", bufs=2))
         psum_t = ctx.enter_context(tc.psum_pool(name="psum_t", bufs=3))
         psum_acc = ctx.enter_context(tc.psum_pool(name="psum_acc", bufs=4))
         psum_s = ctx.enter_context(tc.psum_pool(name="psum_s", bufs=1))
 
-        x_raw = keep.tile([P, GROUPS, TILES_PER_GROUP, H], BF16)
-        w_raw = keep.tile([P, HALVES, BLOCKS_PER_HALF, H], BF16)
+        raw = {"x": keep.tile([P, BLOCKS, H], BF16, name="x_raw"), "w": keep.tile([P, BLOCKS, H], BF16, name="w_raw")}
+        dram = {
+            "x": [x_dram[g, t] for g in range(GROUPS) for t in range(TILES_PER_GROUP)],
+            "w": [w_dram[j] for j in range(BLOCKS)],
+        }
+        codes = {
+            "x": keep.tile([P, PASSES, H], U32, name="x_codes", align_bytes=64),
+            "w": keep.tile([P, PASSES, H], U32, name="w_codes", align_bytes=64),
+        }
+        scales = {
+            "x": keep.tile([P, PASSES, H], U8, name="x_scales", align_bytes=64),
+            "w": keep.tile([P, PASSES, H], U8, name="w_scales", align_bytes=64),
+        }
         vision_rows = keep.tile([P, GROUPS, H], BF16)
         bias_seed = keep.tile([P, H], BF16)
         bias_rows = keep.tile([P, H], BF16)
-        x_codes = keep.tile([P, GROUPS, TILES_PER_GROUP, PASSES * P], U32, align_bytes=64)
-        x_scales = keep.tile([P, GROUPS, TILES_PER_GROUP, PASSES * P], U8, align_bytes=64)
-        w_codes = keep.tile([P, HALVES, PASSES * N_HALF], U32, align_bytes=64)
-        w_scales = keep.tile([P, HALVES, PASSES * N_HALF], U8, align_bytes=64)
 
-        nc.vector.memset(bias_seed[:], 0.0)
-        nc.sync.dma_start(out=bias_seed[0:1, :], in_=bt.unsqueeze(0))
-
-        def load_x(g, t):
-            nc.sync.dma_start(out=x_raw[:, g, t, :], in_=x_dram[g, :, t, :])
-
-        def load_w(half):
-            for j in range(BLOCKS_PER_HALF):
-                nc.sync.dma_start(out=w_raw[:, half, j, :], in_=w_dram[half * BLOCKS_PER_HALF + j])
+        def load(operand, block):
+            nc.sync.dma_start(out=raw[operand][:, block, :], in_=dram[operand][block])
 
         def load_vision(g):
             rows = vision_proj[g * BATCHES_PER_TILE : (g + 1) * BATCHES_PER_TILE, :, :]
@@ -75,21 +79,27 @@ def tile_dynamicroutingfusion_pa_kernel(tc, text_feat, vision_proj, Wt, bt, out_
                 out=vision_rows[:, g, :], in_=rows.to_broadcast([BATCHES_PER_TILE, ROWS_PER_BATCH, H])
             )
 
-        load_x(0, 0)
-        load_w(0)
-        load_vision(0)
-        for t in range(1, TILES_PER_GROUP):
-            load_x(0, t)
-        load_w(1)
-        for g in range(1, GROUPS):
-            for t in range(TILES_PER_GROUP):
-                load_x(g, t)
-            load_vision(g)
+        in_order = [("x", 0)]
+        in_order += [("w", j) for j in range(BLOCKS_PER_HALF)]
+        in_order += [("x", t) for t in range(1, TILES_PER_GROUP)]
+        in_order += [("w", j) for j in range(BLOCKS_PER_HALF, BLOCKS)]
+        in_order += [("x", n) for n in range(TILES_PER_GROUP, BLOCKS)]
+        for operand, block in in_order:
+            load(operand, block)
+            if (operand, block) == ("w", BLOCKS_PER_HALF - 1):
+                load_vision(0)
+            if operand == "x" and block >= TILES_PER_GROUP and block % TILES_PER_GROUP == 0:
+                load_vision(block // TILES_PER_GROUP)
 
+        nc.vector.memset(bias_seed[:], 0.0)
+        nc.scalar.dma_start(out=bias_seed[0:1, :], in_=bt.unsqueeze(0))
         ident = keep.tile([P, P], F32)
         make_identity(nc, ident[:])
         ones = keep.tile([P, P], BF16)
         nc.vector.memset(ones[:], 1.0)
+        warm = keep.tile([P, 1], F32)
+        nc.vector.memset(warm[:], 0.0)
+        nc.scalar.activation(out=warm[:], in_=warm[:], func=ACT.Exp)
         batch_of = keep.tile([P, BATCHES_PER_TILE], F32)
         nc.vector.tensor_reduce(
             out=batch_of[:], in_=ident[:].rearrange("p (b j) -> p b j", j=ROWS_PER_BATCH), axis=AXIS.X, op=ALU.add
@@ -103,60 +113,51 @@ def tile_dynamicroutingfusion_pa_kernel(tc, text_feat, vision_proj, Wt, bt, out_
         nc.vector.tensor_reduce(
             out=place_of[:], in_=ident[:].rearrange("p (b j) -> p j b", j=ROWS_PER_BATCH), axis=AXIS.X, op=ALU.add
         )
-        warm = keep.tile([P, 1], F32)
-        nc.vector.memset(warm[:], 0.0)
-        nc.scalar.activation(out=warm[:], in_=warm[:], func=ACT.Exp)
 
-        bias_bank = psum_t.tile([P, H], BF16, tag="bank")
-        for half in range(HALVES):
-            cols = slice(half * N_HALF, (half + 1) * N_HALF)
-            nc.tensor.matmul(out=bias_bank[:, cols], lhsT=ones[:], rhs=bias_seed[:, cols], start=True, stop=True)
-        nc.scalar.copy(out=bias_rows[:], in_=bias_bank[:])
-
-        def transpose_rows(raw_rows):
-            words = raw_rows.bitcast(F32)
+        def prepare(position):
+            operand, block = in_order[position]
+            words = raw[operand][:, block, :].bitcast(F32)
             bank = psum_t.tile([P, CHUNKS, P], F32, tag="bank")
             for c in range(CHUNKS):
                 nc.tensor.transpose(bank[:, c, :], words[:, c * P : (c + 1) * P], ident[:])
-            return bank[:].rearrange("p (g u) r -> p g r u", u=2)
+            grouped = stage.tile([P, PASSES * P * 4], BF16, align_bytes=64, tag="grouped")
+            grouped_words = grouped[:].bitcast(F32).rearrange("p (g r u) -> p g r u", g=PASSES, u=2)
+            transposed = bank[:].rearrange("p (g u) r -> p g r u", u=2)
+            if position < BLOCKS_BEFORE_FIRST_BANK and position % 2 == 1:
+                nc.vector.tensor_copy(out=grouped_words, in_=transposed)
+            else:
+                nc.scalar.copy(out=grouped_words, in_=transposed)
+            return grouped
 
-        def prepare_x(g, t):
-            grouped = stage.tile([P, PASSES * P * 4], BF16, align_bytes=64, tag="grouped_x")
-            nc.scalar.copy(
-                out=grouped[:].bitcast(F32).rearrange("p (g r u) -> p g r u", g=PASSES, u=2),
-                in_=transpose_rows(x_raw[:, g, t, :]),
-            )
-            nc.vector.quantize_mx(out=x_codes[:, g, t, :].bitcast(FP8X4), scales=x_scales[:, g, t, :], in_=grouped[:])
-
-        def prepare_w(half):
-            grouped = stage.tile([P, PASSES * N_HALF * 4], BF16, align_bytes=64, tag="grouped_w", bufs=2)
-            grouped_words = grouped[:].bitcast(F32).rearrange("p (g n u) -> p g n u", g=PASSES, u=2)
-            for j in range(BLOCKS_PER_HALF):
-                transposed = transpose_rows(w_raw[:, half, j, :])
-                if j % 2 == 0:
-                    nc.scalar.copy(out=grouped_words[:, :, j * P : (j + 1) * P, :], in_=transposed)
-                else:
-                    nc.vector.tensor_copy(out=grouped_words[:, :, j * P : (j + 1) * P, :], in_=transposed)
+        def quantise(position, grouped):
+            operand, block = in_order[position]
             for c in range(PASSES):
                 nc.vector.quantize_mx(
-                    out=w_codes[:, half, c * N_HALF : (c + 1) * N_HALF].bitcast(FP8X4),
-                    scales=w_scales[:, half, c * N_HALF : (c + 1) * N_HALF],
-                    in_=grouped[:, c * N_HALF * 4 : (c + 1) * N_HALF * 4],
+                    out=codes[operand][:, c, block * P : (block + 1) * P].bitcast(FP8X4),
+                    scales=scales[operand][:, c, block * P : (block + 1) * P],
+                    in_=grouped[:, c * P * 4 : (c + 1) * P * 4],
                 )
 
-        def project(g, t, half, coupling_parts):
-            cols = slice(half * N_HALF, (half + 1) * N_HALF)
+        def positions_from(first):
+            return range(first, min(first + BLOCKS_PER_BANK, len(in_order)))
+
+        def multiply(g, half, t):
+            block = g * TILES_PER_GROUP + t
             acc = psum_acc.tile([P, N_HALF], F32)
             for c in range(PASSES):
                 nc.tensor.matmul_mx(
                     out=acc[:],
-                    lhsT=x_codes[:, g, t, c * P : (c + 1) * P].bitcast(FP8X4),
-                    lhsT_scale=x_scales[:, g, t, c * P : (c + 1) * P],
-                    rhs=w_codes[:, half, c * N_HALF : (c + 1) * N_HALF].bitcast(FP8X4),
-                    rhs_scale=w_scales[:, half, c * N_HALF : (c + 1) * N_HALF],
+                    lhsT=codes["x"][:, c, block * P : (block + 1) * P].bitcast(FP8X4),
+                    lhsT_scale=scales["x"][:, c, block * P : (block + 1) * P],
+                    rhs=codes["w"][:, c, half * N_HALF : (half + 1) * N_HALF].bitcast(FP8X4),
+                    rhs_scale=scales["w"][:, c, half * N_HALF : (half + 1) * N_HALF],
                     start=(c == 0),
                     stop=(c == PASSES - 1),
                 )
+            return acc
+
+        def finish(g, half, t, acc, coupling_parts, proj):
+            cols = slice(half * N_HALF, (half + 1) * N_HALF)
             product = stage.tile([P, N_HALF], F32, tag="product")
             nc.vector.scalar_tensor_tensor(
                 out=product[:],
@@ -167,11 +168,16 @@ def tile_dynamicroutingfusion_pa_kernel(tc, text_feat, vision_proj, Wt, bt, out_
                 op1=ALU.mult,
                 accum_out=coupling_parts[:, half, t : t + 1],
             )
-            proj = results.tile([P, N_HALF], F32, tag="proj")
-            nc.vector.tensor_tensor(out=proj[:], in0=acc[:], in1=bias_rows[:, cols], op=ALU.add)
-            nc.sync.dma_start(out=proj_dram[g, :, t, cols], in_=proj[:])
+            if half == 0:
+                nc.vector.tensor_tensor(out=proj[:, cols], in0=acc[:], in1=bias_rows[:, cols], op=ALU.add)
+            else:
+                bare = stage.tile([P, N_HALF], F32, tag="bare")
+                nc.scalar.copy(out=bare[:], in_=acc[:])
+                nc.gpsimd.tensor_tensor(out=proj[:, cols], in0=bare[:], in1=bias_rows[:, cols], op=ALU.add)
+            if half == HALVES - 1:
+                nc.sync.dma_start(out=proj_dram[g, t], in_=proj[:])
 
-        def route(g, coupling_parts):
+        def spread_couplings(coupling_parts):
             coupling = small.tile([P, TILES_PER_GROUP], F32, tag="coupling")
             nc.vector.tensor_tensor(out=coupling[:], in0=coupling_parts[:, 0, :], in1=coupling_parts[:, 1, :], op=ALU.add)
             spread = small.tile([P, TILES_PER_GROUP, ROWS_PER_BATCH], F32, tag="spread")
@@ -181,40 +187,102 @@ def tile_dynamicroutingfusion_pa_kernel(tc, text_feat, vision_proj, Wt, bt, out_
                 in1=place_of[:].unsqueeze(1).to_broadcast([P, TILES_PER_GROUP, ROWS_PER_BATCH]),
                 op=ALU.mult,
             )
+            return {"coupling": coupling, "spread": spread}
+
+        def gather_couplings(state):
             batch_couplings = psum_s.tile([P, TOKENS], F32)
             nc.tensor.matmul(
-                out=batch_couplings[:], lhsT=same_batch[:], rhs=spread[:].rearrange("p t j -> p (t j)"), start=True, stop=True
+                out=batch_couplings[:],
+                lhsT=same_batch[:],
+                rhs=state["spread"][:].rearrange("p t j -> p (t j)"),
+                start=True,
+                stop=True,
             )
+            state["batch_couplings"] = batch_couplings
+
+        def exponentials(state):
             minus_max = small.tile([P, 1], F32, tag="minus_max")
-            nc.vector.tensor_reduce(out=minus_max[:], in_=batch_couplings[:], axis=AXIS.X, op=ALU.max, negate=True)
+            nc.vector.tensor_reduce(
+                out=minus_max[:], in_=state["batch_couplings"][:], axis=AXIS.X, op=ALU.max, negate=True
+            )
             exp_all = small.tile([P, TOKENS], F32, tag="exp_all")
             exp_sum = small.tile([P, 1], F32, tag="exp_sum")
             nc.scalar.activation(
-                out=exp_all[:], in_=batch_couplings[:], func=ACT.Exp, bias=minus_max[:], scale=1.0, accum_out=exp_sum[:]
+                out=exp_all[:],
+                in_=state["batch_couplings"][:],
+                func=ACT.Exp,
+                bias=minus_max[:],
+                scale=1.0,
+                accum_out=exp_sum[:],
             )
             exp_own = small.tile([P, TILES_PER_GROUP], F32, tag="exp_own")
-            nc.scalar.activation(out=exp_own[:], in_=coupling[:], func=ACT.Exp, bias=minus_max[:], scale=1.0)
+            nc.scalar.activation(out=exp_own[:], in_=state["coupling"][:], func=ACT.Exp, bias=minus_max[:], scale=1.0)
+            state["exp_sum"] = exp_sum
+            state["exp_own"] = exp_own
+
+        def normalise(state):
             inverse_sum = small.tile([P, 1], F32, tag="inverse_sum")
-            nc.vector.reciprocal(out=inverse_sum[:], in_=exp_sum[:])
+            nc.vector.reciprocal(out=inverse_sum[:], in_=state["exp_sum"][:])
             routing = small.tile([P, TILES_PER_GROUP], F32, tag="routing")
-            nc.vector.tensor_scalar(out=routing[:], in0=exp_own[:], scalar1=inverse_sum[:, 0:1], scalar2=None, op0=ALU.mult)
-            for t in range(TILES_PER_GROUP):
-                weighted = results.tile([P, H], F32, tag="weighted", bufs=4)
-                nc.scalar.activation(out=weighted[:], in_=vision_rows[:, g, :], func=ACT.Copy, scale=routing[:, t : t + 1])
-                nc.sync.dma_start(out=weighted_dram[g, :, t, :], in_=weighted[:])
+            nc.vector.tensor_scalar(
+                out=routing[:], in0=state["exp_own"][:], scalar1=inverse_sum[:, 0:1], scalar2=None, op0=ALU.mult
+            )
+            state["routing"] = routing
 
-        prepare_x(0, 0)
-        prepare_w(0)
-        for t in range(1, TILES_PER_GROUP):
-            prepare_x(0, t)
-        prepare_w(1)
-        for g in range(1, GROUPS):
-            for t in range(TILES_PER_GROUP):
-                prepare_x(g, t)
+        def weigh(g, t, state):
+            weight = state["routing"][:, t : t + 1]
+            weighted = results.tile([P, H], F32, tag="weighted")
+            nc.scalar.activation(out=weighted[:, 0:N_HALF], in_=vision_rows[:, g, 0:N_HALF], func=ACT.Copy, scale=weight)
+            nc.gpsimd.tensor_scalar(
+                out=weighted[:, N_HALF:H],
+                in0=vision_rows[:, g, N_HALF:H],
+                scalar1=weight,
+                scalar2=0.0,
+                op0=ALU.mult,
+                op1=ALU.add,
+            )
+            nc.sync.dma_start(out=weighted_dram[g, t], in_=weighted[:])
 
-        for g in range(GROUPS):
-            coupling_parts = small.tile([P, HALVES, TILES_PER_GROUP], F32, tag="coupling_parts")
-            for half in range(HALVES):
-                for t in range(TILES_PER_GROUP):
-                    project(g, t, half, coupling_parts)
-            route(g, coupling_parts)
+        banks = [(0, half, t) for half in range(HALVES) for t in range(TILES_PER_GROUP)]
+        banks += [(g, half, t) for g in range(1, GROUPS) for t in range(TILES_PER_GROUP) for half in range(HALVES)]
+        coupling_parts = [small.tile([P, HALVES, TILES_PER_GROUP], F32, name="coupling_parts") for g in range(GROUPS)]
+
+        for first in range(0, BLOCKS_BEFORE_FIRST_BANK, BLOCKS_PER_BANK):
+            grouped_tiles = [prepare(position) for position in positions_from(first)]
+            for position, grouped in zip(positions_from(first), grouped_tiles):
+                quantise(position, grouped)
+        bias_bank = psum_t.tile([P, H], BF16, tag="bank")
+        for half in range(HALVES):
+            cols = slice(half * N_HALF, (half + 1) * N_HALF)
+            nc.tensor.matmul(out=bias_bank[:, cols], lhsT=ones[:], rhs=bias_seed[:, cols], start=True, stop=True)
+        nc.scalar.copy(out=bias_rows[:], in_=bias_bank[:])
+        acc = multiply(0, 0, 0)
+
+        state = None
+        proj_tiles = None
+        for i in range(len(banks)):
+            g, half, t = banks[i]
+            bank_number = i % (HALVES * TILES_PER_GROUP)
+            if bank_number == 0:
+                proj_tiles = [results.tile([P, H], F32, name="proj", tag="proj") for n in range(TILES_PER_GROUP)]
+            first = BLOCKS_BEFORE_FIRST_BANK + i * BLOCKS_PER_BANK
+            grouped_tiles = [prepare(position) for position in positions_from(first)]
+            finish(g, half, t, acc, coupling_parts[g], proj_tiles[t])
+            for position, grouped in zip(positions_from(first), grouped_tiles):
+                quantise(position, grouped)
+            if i + 1 < len(banks):
+                acc = multiply(banks[i + 1][0], banks[i + 1][1], banks[i + 1][2])
+            if g > 0 and bank_number == 0:
+                gather_couplings(state)
+                exponentials(state)
+            if g > 0 and bank_number == 1:
+                normalise(state)
+            if g > 0 and 2 <= bank_number < 2 + TILES_PER_GROUP:
+                weigh(g - 1, bank_number - 2, state)
+            if bank_number == HALVES * TILES_PER_GROUP - 1:
+                state = spread_couplings(coupling_parts[g])
+        gather_couplings(state)
+        exponentials(state)
+        normalise(state)
+        for t in range(TILES_PER_GROUP):
+            weigh(GROUPS - 1, t, state)

@@ -179,9 +179,9 @@ def tile_dynamicroutingfusion_pa_kernel(tc, text_feat, vision_proj, Wt, bt, out_
 
         def spread_couplings(coupling_parts):
             coupling = small.tile([P, TILES_PER_GROUP], F32, tag="coupling")
-            nc.vector.tensor_tensor(out=coupling[:], in0=coupling_parts[:, 0, :], in1=coupling_parts[:, 1, :], op=ALU.add)
+            nc.gpsimd.tensor_tensor(out=coupling[:], in0=coupling_parts[:, 0, :], in1=coupling_parts[:, 1, :], op=ALU.add)
             spread = small.tile([P, TILES_PER_GROUP, ROWS_PER_BATCH], F32, tag="spread")
-            nc.vector.tensor_tensor(
+            nc.gpsimd.tensor_tensor(
                 out=spread[:],
                 in0=coupling[:].unsqueeze(2).to_broadcast([P, TILES_PER_GROUP, ROWS_PER_BATCH]),
                 in1=place_of[:].unsqueeze(1).to_broadcast([P, TILES_PER_GROUP, ROWS_PER_BATCH]),
@@ -224,8 +224,13 @@ def tile_dynamicroutingfusion_pa_kernel(tc, text_feat, vision_proj, Wt, bt, out_
             inverse_sum = small.tile([P, 1], F32, tag="inverse_sum")
             nc.vector.reciprocal(out=inverse_sum[:], in_=state["exp_sum"][:])
             routing = small.tile([P, TILES_PER_GROUP], F32, tag="routing")
-            nc.vector.tensor_scalar(
-                out=routing[:], in0=state["exp_own"][:], scalar1=inverse_sum[:, 0:1], scalar2=None, op0=ALU.mult
+            nc.gpsimd.tensor_scalar(
+                out=routing[:],
+                in0=state["exp_own"][:],
+                scalar1=inverse_sum[:, 0:1],
+                scalar2=0.0,
+                op0=ALU.mult,
+                op1=ALU.add,
             )
             state["routing"] = routing
 

from contextlib import ExitStack

import concourse.mybir as mybir
from concourse.masks import make_identity

F32 = mybir.dt.float32
BF16 = mybir.dt.bfloat16
U32 = mybir.dt.uint32
U8 = mybir.dt.uint8
FP8X4 = mybir.dt.float8_e4m3fn_x4
ALU = mybir.AluOpType
ACT = mybir.ActivationFunctionType
AXIS = mybir.AxisListType

P = 128
BATCH = 32
TOKENS = 32
H = 1024

K_PASS = 4 * P
PASSES = H // K_PASS
CHUNKS = H // (2 * P)
N_HALF = 512
HALVES = H // N_HALF
BLOCKS = H // P
BLOCKS_PER_HALF = N_HALF // P

BATCHES_PER_TILE = 8
ROWS_PER_BATCH = P // BATCHES_PER_TILE
TILES_PER_GROUP = TOKENS // ROWS_PER_BATCH
GROUPS = BATCH // BATCHES_PER_TILE

BLOCKS_BEFORE_FIRST_BANK = 1 + BLOCKS_PER_HALF + 1
BLOCKS_PER_BANK = 2

FLOPS = 2 * BATCH * TOKENS * H * H


def tile_dynamicroutingfusion_pa_kernel(tc, text_feat, vision_proj, Wt, bt, out_0, out_1):
    nc = tc.nc

    x_dram = text_feat.flatten_outer_dims().rearrange("(g p t) k -> g t p k", p=P, t=TILES_PER_GROUP)
    proj_dram = out_0.flatten_outer_dims().rearrange("(g p t) h -> g t p h", p=P, t=TILES_PER_GROUP)
    weighted_dram = out_1.flatten_outer_dims().rearrange("(g p t) h -> g t p h", p=P, t=TILES_PER_GROUP)
    w_dram = Wt.rearrange("(j p) k -> j p k", p=P)

    with ExitStack() as ctx:
        keep = ctx.enter_context(tc.tile_pool(name="keep", bufs=1))
        stage = ctx.enter_context(tc.tile_pool(name="stage", bufs=4))
        results = ctx.enter_context(tc.tile_pool(name="results", bufs=2 * TILES_PER_GROUP))
        small = ctx.enter_context(tc.tile_pool(name="small", bufs=2))
        psum_t = ctx.enter_context(tc.psum_pool(name="psum_t", bufs=3))
        psum_acc = ctx.enter_context(tc.psum_pool(name="psum_acc", bufs=4))
        psum_s = ctx.enter_context(tc.psum_pool(name="psum_s", bufs=1))

        raw = {"x": keep.tile([P, BLOCKS, H], BF16, name="x_raw"), "w": keep.tile([P, BLOCKS, H], BF16, name="w_raw")}
        dram = {
            "x": [x_dram[g, t] for g in range(GROUPS) for t in range(TILES_PER_GROUP)],
            "w": [w_dram[j] for j in range(BLOCKS)],
        }
        codes = {
            "x": keep.tile([P, PASSES, H], U32, name="x_codes", align_bytes=64),
            "w": keep.tile([P, PASSES, H], U32, name="w_codes", align_bytes=64),
        }
        scales = {
            "x": keep.tile([P, PASSES, H], U8, name="x_scales", align_bytes=64),
            "w": keep.tile([P, PASSES, H], U8, name="w_scales", align_bytes=64),
        }
        vision_rows = keep.tile([P, GROUPS, H], BF16)
        bias_seed = keep.tile([P, H], BF16)
        bias_rows = keep.tile([P, H], BF16)

        def load(operand, block):
            nc.sync.dma_start(out=raw[operand][:, block, :], in_=dram[operand][block])

        def load_vision(g):
            rows = vision_proj[g * BATCHES_PER_TILE : (g + 1) * BATCHES_PER_TILE, :, :]
            nc.sync.dma_start(
                out=vision_rows[:, g, :], in_=rows.to_broadcast([BATCHES_PER_TILE, ROWS_PER_BATCH, H])
            )

        in_order = [("x", 0)]
        in_order += [("w", j) for j in range(BLOCKS_PER_HALF)]
        in_order += [("x", t) for t in range(1, TILES_PER_GROUP)]
        in_order += [("w", j) for j in range(BLOCKS_PER_HALF, BLOCKS)]
        in_order += [("x", n) for n in range(TILES_PER_GROUP, BLOCKS)]
        for operand, block in in_order:
            load(operand, block)
            if (operand, block) == ("w", BLOCKS_PER_HALF - 1):
                load_vision(0)
            if operand == "x" and block >= TILES_PER_GROUP and block % TILES_PER_GROUP == 0:
                load_vision(block // TILES_PER_GROUP)

        nc.vector.memset(bias_seed[:], 0.0)
        nc.scalar.dma_start(out=bias_seed[0:1, :], in_=bt.unsqueeze(0))
        ident = keep.tile([P, P], F32)
        make_identity(nc, ident[:])
        ones = keep.tile([P, P], BF16)
        nc.vector.memset(ones[:], 1.0)
        warm = keep.tile([P, 1], F32)
        nc.vector.memset(warm[:], 0.0)
        nc.scalar.activation(out=warm[:], in_=warm[:], func=ACT.Exp)
        batch_of = keep.tile([P, BATCHES_PER_TILE], F32)
        nc.vector.tensor_reduce(
            out=batch_of[:], in_=ident[:].rearrange("p (b j) -> p b j", j=ROWS_PER_BATCH), axis=AXIS.X, op=ALU.add
        )
        same_batch = keep.tile([P, P], F32)
        nc.vector.tensor_copy(
            out=same_batch[:].rearrange("p (b j) -> p b j", j=ROWS_PER_BATCH),
            in_=batch_of[:].unsqueeze(2).to_broadcast([P, BATCHES_PER_TILE, ROWS_PER_BATCH]),
        )
        place_of = keep.tile([P, ROWS_PER_BATCH], F32)
        nc.vector.tensor_reduce(
            out=place_of[:], in_=ident[:].rearrange("p (b j) -> p j b", j=ROWS_PER_BATCH), axis=AXIS.X, op=ALU.add
        )

        def prepare(position):
            operand, block = in_order[position]
            words = raw[operand][:, block, :].bitcast(F32)
            bank = psum_t.tile([P, CHUNKS, P], F32, tag="bank")
            for c in range(CHUNKS):
                nc.tensor.transpose(bank[:, c, :], words[:, c * P : (c + 1) * P], ident[:])
            grouped = stage.tile([P, PASSES * P * 4], BF16, align_bytes=64, tag="grouped")
            grouped_words = grouped[:].bitcast(F32).rearrange("p (g r u) -> p g r u", g=PASSES, u=2)
            transposed = bank[:].rearrange("p (g u) r -> p g r u", u=2)
            if position < BLOCKS_BEFORE_FIRST_BANK and position % 2 == 1:
                nc.vector.tensor_copy(out=grouped_words, in_=transposed)
            else:
                nc.scalar.copy(out=grouped_words, in_=transposed)
            return grouped

        def quantise(position, grouped):
            operand, block = in_order[position]
            for c in range(PASSES):
                nc.vector.quantize_mx(
                    out=codes[operand][:, c, block * P : (block + 1) * P].bitcast(FP8X4),
                    scales=scales[operand][:, c, block * P : (block + 1) * P],
                    in_=grouped[:, c * P * 4 : (c + 1) * P * 4],
                )

        def positions_from(first):
            return range(first, min(first + BLOCKS_PER_BANK, len(in_order)))

        def multiply(g, half, t):
            block = g * TILES_PER_GROUP + t
            acc = psum_acc.tile([P, N_HALF], F32)
            for c in range(PASSES):
                nc.tensor.matmul_mx(
                    out=acc[:],
                    lhsT=codes["x"][:, c, block * P : (block + 1) * P].bitcast(FP8X4),
                    lhsT_scale=scales["x"][:, c, block * P : (block + 1) * P],
                    rhs=codes["w"][:, c, half * N_HALF : (half + 1) * N_HALF].bitcast(FP8X4),
                    rhs_scale=scales["w"][:, c, half * N_HALF : (half + 1) * N_HALF],
                    start=(c == 0),
                    stop=(c == PASSES - 1),
                )
            return acc

        def finish(g, half, t, acc, coupling_parts, proj):
            cols = slice(half * N_HALF, (half + 1) * N_HALF)
            product = stage.tile([P, N_HALF], F32, tag="product")
            nc.vector.scalar_tensor_tensor(
                out=product[:],
                in0=acc[:],
                scalar=2.0,
                in1=vision_rows[:, g, cols],
                op0=ALU.mult,
                op1=ALU.mult,
                accum_out=coupling_parts[:, half, t : t + 1],
            )
            if half == 0:
                nc.vector.tensor_tensor(out=proj[:, cols], in0=acc[:], in1=bias_rows[:, cols], op=ALU.add)
            else:
                bare = stage.tile([P, N_HALF], F32, tag="bare")
                nc.scalar.copy(out=bare[:], in_=acc[:])
                nc.gpsimd.tensor_tensor(out=proj[:, cols], in0=bare[:], in1=bias_rows[:, cols], op=ALU.add)
            if half == HALVES - 1:
                nc.sync.dma_start(out=proj_dram[g, t], in_=proj[:])

        def spread_couplings(coupling_parts):
            coupling = small.tile([P, TILES_PER_GROUP], F32, tag="coupling")
            nc.gpsimd.tensor_tensor(out=coupling[:], in0=coupling_parts[:, 0, :], in1=coupling_parts[:, 1, :], op=ALU.add)
            spread = small.tile([P, TILES_PER_GROUP, ROWS_PER_BATCH], F32, tag="spread")
            nc.gpsimd.tensor_tensor(
                out=spread[:],
                in0=coupling[:].unsqueeze(2).to_broadcast([P, TILES_PER_GROUP, ROWS_PER_BATCH]),
                in1=place_of[:].unsqueeze(1).to_broadcast([P, TILES_PER_GROUP, ROWS_PER_BATCH]),
                op=ALU.mult,
            )
            return {"coupling": coupling, "spread": spread}

        def gather_couplings(state):
            batch_couplings = psum_s.tile([P, TOKENS], F32)
            nc.tensor.matmul(
                out=batch_couplings[:],
                lhsT=same_batch[:],
                rhs=state["spread"][:].rearrange("p t j -> p (t j)"),
                start=True,
                stop=True,
            )
            state["batch_couplings"] = batch_couplings

        def exponentials(state):
            minus_max = small.tile([P, 1], F32, tag="minus_max")
            nc.vector.tensor_reduce(
                out=minus_max[:], in_=state["batch_couplings"][:], axis=AXIS.X, op=ALU.max, negate=True
            )
            exp_all = small.tile([P, TOKENS], F32, tag="exp_all")
            exp_sum = small.tile([P, 1], F32, tag="exp_sum")
            nc.scalar.activation(
                out=exp_all[:],
                in_=state["batch_couplings"][:],
                func=ACT.Exp,
                bias=minus_max[:],
                scale=1.0,
                accum_out=exp_sum[:],
            )
            exp_own = small.tile([P, TILES_PER_GROUP], F32, tag="exp_own")
            nc.scalar.activation(out=exp_own[:], in_=state["coupling"][:], func=ACT.Exp, bias=minus_max[:], scale=1.0)
            state["exp_sum"] = exp_sum
            state["exp_own"] = exp_own

        def normalise(state):
            inverse_sum = small.tile([P, 1], F32, tag="inverse_sum")
            nc.vector.reciprocal(out=inverse_sum[:], in_=state["exp_sum"][:])
            routing = small.tile([P, TILES_PER_GROUP], F32, tag="routing")
            nc.gpsimd.tensor_scalar(
                out=routing[:],
                in0=state["exp_own"][:],
                scalar1=inverse_sum[:, 0:1],
                scalar2=0.0,
                op0=ALU.mult,
                op1=ALU.add,
            )
            state["routing"] = routing

        def weigh(g, t, state):
            weight = state["routing"][:, t : t + 1]
            weighted = results.tile([P, H], F32, tag="weighted")
            nc.scalar.activation(out=weighted[:, 0:N_HALF], in_=vision_rows[:, g, 0:N_HALF], func=ACT.Copy, scale=weight)
            nc.gpsimd.tensor_scalar(
                out=weighted[:, N_HALF:H],
                in0=vision_rows[:, g, N_HALF:H],
                scalar1=weight,
                scalar2=0.0,
                op0=ALU.mult,
                op1=ALU.add,
            )
            nc.sync.dma_start(out=weighted_dram[g, t], in_=weighted[:])

        banks = [(0, half, t) for half in range(HALVES) for t in range(TILES_PER_GROUP)]
        banks += [(g, half, t) for g in range(1, GROUPS) for t in range(TILES_PER_GROUP) for half in range(HALVES)]
        coupling_parts = [small.tile([P, HALVES, TILES_PER_GROUP], F32, name="coupling_parts") for g in range(GROUPS)]

        for first in range(0, BLOCKS_BEFORE_FIRST_BANK, BLOCKS_PER_BANK):
            grouped_tiles = [prepare(position) for position in positions_from(first)]
            for position, grouped in zip(positions_from(first), grouped_tiles):
                quantise(position, grouped)
        bias_bank = psum_t.tile([P, H], BF16, tag="bank")
        for half in range(HALVES):
            cols = slice(half * N_HALF, (half + 1) * N_HALF)
            nc.tensor.matmul(out=bias_bank[:, cols], lhsT=ones[:], rhs=bias_seed[:, cols], start=True, stop=True)
        nc.scalar.copy(out=bias_rows[:], in_=bias_bank[:])
        acc = multiply(0, 0, 0)

        state = None
        proj_tiles = None
        for i in range(len(banks)):
            g, half, t = banks[i]
            bank_number = i % (HALVES * TILES_PER_GROUP)
            if bank_number == 0:
                proj_tiles = [results.tile([P, H], F32, name="proj", tag="proj") for n in range(TILES_PER_GROUP)]
            first = BLOCKS_BEFORE_FIRST_BANK + i * BLOCKS_PER_BANK
            grouped_tiles = [prepare(position) for position in positions_from(first)]
            finish(g, half, t, acc, coupling_parts[g], proj_tiles[t])
            for position, grouped in zip(positions_from(first), grouped_tiles):
                quantise(position, grouped)
            if i + 1 < len(banks):
                acc = multiply(banks[i + 1][0], banks[i + 1][1], banks[i + 1][2])
            if g > 0 and bank_number == 0:
                gather_couplings(state)
                exponentials(state)
            if g > 0 and bank_number == 1:
                normalise(state)
            if g > 0 and 2 <= bank_number < 2 + TILES_PER_GROUP:
                weigh(g - 1, bank_number - 2, state)
            if bank_number == HALVES * TILES_PER_GROUP - 1:
                state = spread_couplings(coupling_parts[g])
        gather_couplings(state)
        exponentials(state)
        normalise(state)
        for t in range(TILES_PER_GROUP):
            weigh(GROUPS - 1, t, state)
